import numpy as np
import ml_dtypes


def mxq(x, axis, fmt="e4m3"):
    dtype, down = {"e4m3": (ml_dtypes.float8_e4m3fn, 7), "e5m2": (ml_dtypes.float8_e5m2, 14)}[fmt]
    v = np.moveaxis(np.asarray(x, np.float32).astype(ml_dtypes.bfloat16).astype(np.float64), axis, -1)
    blocks = v.reshape(v.shape[:-1] + (-1, 32))
    amax = np.abs(blocks).max(-1, keepdims=True)
    byte = np.maximum(np.where(amax > 0, np.frexp(amax)[1] - 1 + 127, 0) - down, 1)
    scale = np.exp2(byte - 127.0)
    codes = (blocks / scale).astype(np.float32).astype(dtype).astype(np.float64)
    return np.moveaxis((codes * scale).reshape(v.shape), -1, axis)


WIDE = False


def mx_kscale(k):
    if not WIDE:
        return np.ones(k)
    levels = np.array([10, -10, 5, -5, 0])
    a = np.random.permutation(np.resize(levels, k // 512 * 4)).reshape(k // 512, 4)
    idx = np.arange(k)
    return np.exp2(a[idx // 512, idx % 128 // 32])


BF16 = ml_dtypes.bfloat16


def bf(x):
    return np.asarray(x, np.float32).astype(BF16)


def f64(x):
    return np.asarray(x).astype(np.float64)


E2M1 = np.array([0.0, 0.5, 1.0, 1.5, 2.0, 3.0, 4.0, 6.0, -0.0, -0.5, -1.0, -1.5, -2.0, -3.0, -4.0, -6.0])


def pack_weight(w, fmt):
    k, n = w.shape
    w = f64(bf(w)).reshape(k // 32, 32, n)
    amax = np.abs(w).max(1)
    if fmt == "e4m3":
        byte = np.frexp(amax)[1] - 1 + 127 - 7
    else:
        mant, ex = np.frexp(amax / 6.0)
        byte = np.where(mant > 0.5, ex, ex - 1) + 127
    byte = np.clip(np.where(amax > 0, byte, 1), 1, 254)
    scaled = (w * np.exp2(127.0 - byte)[:, None, :]).reshape(k, n).astype(np.float32)
    by_word = np.ascontiguousarray(scaled.reshape(k // 512, 128, 4, n).transpose(0, 1, 3, 2))
    if fmt == "e4m3":
        words = by_word.astype(ml_dtypes.float8_e4m3fn).view(np.uint8)
    else:
        c = by_word.astype(ml_dtypes.float4_e2m1fn).view(np.uint8) & 0xF
        words = c[..., 0::2] | (c[..., 1::2] << 4)
    return np.ascontiguousarray(words), np.ascontiguousarray(byte.astype(np.uint8).reshape(k // 512, 16, n))


def unpack_weight(words, scales, fmt):
    g, p, n, _ = words.shape
    if fmt == "e4m3":
        vals = np.ascontiguousarray(words).view(ml_dtypes.float8_e4m3fn).astype(np.float64)
    else:
        nib = np.empty((g, p, n, 4), np.uint8)
        nib[..., 0::2] = words & 0xF
        nib[..., 1::2] = words >> 4
        vals = E2M1[nib]
    vals = vals * np.repeat(np.exp2(scales.astype(np.float64) - 127.0), 8, axis=1)[..., None]
    return vals.transpose(0, 1, 3, 2).reshape(g * 512, n)

def pack4(w):
    words, scales = pack_weight(w, "e2m1")
    return words.reshape(words.shape[0], 128, -1), scales


def unpack4(words, scales):
    return unpack_weight(words.reshape(words.shape[0], 128, -1, 2), scales, "e2m1")


B, D, L, H = 8192, 512, 128, 1024


def sigmoid(v):
    return 1.0 / (1.0 + np.exp(-v))


def setup_inputs():
    t = mx_kscale(H)
    z = bf(np.random.standard_normal((B, L)) * 1.7)
    x = bf(np.random.random((B, D)) < 0.5)
    Wd1 = bf(np.random.standard_normal((L, H)) * 0.6 / np.sqrt(L) * t)
    bd1 = bf(np.random.standard_normal(H) * 0.5 * t)
    Wd2_words, Wd2_scales = pack4(np.random.standard_normal((H, D)) * 2.8 / np.sqrt(H) / t[:, None])
    bd2 = bf(np.random.standard_normal(D) * 0.5)
    return {
        "z": z,
        "x": x,
        "Wd1": Wd1,
        "bd1": bd1,
        "Wd2_words": Wd2_words,
        "Wd2_scales": Wd2_scales,
        "bd2": bd2,
    }


def reference(z, x, Wd1, bd1, Wd2_words, Wd2_scales, bd2):
    x = f64(x)
    hd = np.maximum(f64(z) @ f64(Wd1) + f64(bd1), 0.0)
    theta = sigmoid((mxq(hd, 1, "e4m3") @ unpack4(Wd2_words, Wd2_scales)) + f64(bd2))
    return np.sum(x * np.log(theta) + (1.0 - x) * np.log1p(-theta), axis=-1)

@@ -1,0 +1,250 @@
+from contextlib import ExitStack
+
+import concourse.mybir as mybir
+from concourse.masks import make_identity
+
+F32 = mybir.dt.float32
+BF16 = mybir.dt.bfloat16
+I32 = mybir.dt.int32
+U32 = mybir.dt.uint32
+U8 = mybir.dt.uint8
+FP8X4 = mybir.dt.float8_e4m3fn_x4
+FP4X4 = mybir.dt.float4_e2m1fn_x4
+ACT = mybir.ActivationFunctionType
+ALU = mybir.AluOpType
+
+P = 128
+B, D, L, H = 8192, 512, 128, 1024
+PACK = 4
+K_PASS = P * PACK
+GROUPS = H // K_PASS
+TILES = B // P
+BLOCK = 4
+BLOCKS = TILES // BLOCK
+COLS = BLOCK * P
+Z_CHUNK = 4
+SUPER = 4
+
+FLOPS = 2 * B * L * H + 2 * B * H * D
+
+
+def tile_vae_pb_t_kernel(tc, z, x, Wd1, bd1, Wd2_words, Wd2_scales, bd2, out):
+    nc = tc.nc
+    z_rows = z.rearrange("(p i) l -> p i l", i=TILES)
+    x_rows = x.rearrange("(p i) j -> p i j", i=TILES)
+    out_rows = out.rearrange("(p i) -> p i", i=TILES)
+
+    with ExitStack() as ctx:
+        const = ctx.enter_context(tc.tile_pool(name="const", bufs=1))
+        work = ctx.enter_context(tc.tile_pool(name="work", bufs=3))
+        psum_t = ctx.enter_context(tc.psum_pool(name="psum_t", bufs=1))
+        psum_h = ctx.enter_context(tc.psum_pool(name="psum_h", bufs=4))
+        psum_v = ctx.enter_context(tc.psum_pool(name="psum_v", bufs=3))
+        ctx.enter_context(tc.manual_schedule())
+
+        w2_scales = const.tile([P, GROUPS, D], U8, align_bytes=64)
+        nc.vector.memset(w2_scales[:].bitcast(I32), 0)
+        one = const.tile([P, 1], F32)
+        nc.vector.memset(one[:], 1.0)
+        ident = const.tile([P, P], BF16)
+        make_identity(nc, ident[:])
+
+        z_sb = {}
+        x_sb = {}
+
+        def load_z(c):
+            z_chunk = const.tile([P, Z_CHUNK * BLOCK, L], BF16, name="z%d" % c)
+            first = c * Z_CHUNK * BLOCK
+            nc.sync.dma_start(out=z_chunk[:], in_=z_rows[:, first : first + Z_CHUNK * BLOCK, :])
+            z_sb[c] = z_chunk
+
+        def load_x(k):
+            x_block = const.tile([P, BLOCK, D], BF16, name="x%d" % k)
+            nc.sync.dma_start(out=x_block[:], in_=x_rows[:, k * BLOCK : (k + 1) * BLOCK, :])
+            x_sb[k] = x_block
+
+        load_z(0)
+        w1_sb = const.tile([P, H], BF16)
+        nc.sync.dma_start(out=w1_sb[:], in_=Wd1)
+        b1_bf = const.tile([P, GROUPS, PACK], BF16)
+        nc.sync.dma_start(out=b1_bf[:], in_=bd1.rearrange("(g p t) -> p g t", g=GROUPS, t=PACK))
+        w2_words = const.tile([P, GROUPS, 2 * D], U8, align_bytes=64)
+        for g in range(GROUPS):
+            nc.sync.dma_start(out=w2_words[:, g, :].bitcast(I32), in_=Wd2_words[g].bitcast(I32))
+        for quad in range(4):
+            nc.sync.dma_start(
+                out=w2_scales[32 * quad : 32 * quad + 4].bitcast(I32),
+                in_=Wd2_scales[:, 4 * quad : 4 * quad + 4, :].bitcast(I32).rearrange("g r n -> r g n"),
+            )
+        b2_all = const.tile([P, D], BF16)
+        nc.sync.dma_start(out=b2_all[:], in_=bd2.partition_broadcast(P))
+        for k in range(BLOCKS):
+            load_x(k)
+            if k % Z_CHUNK == 1 and k // Z_CHUNK + 1 < BLOCKS // Z_CHUNK:
+                load_z(k // Z_CHUNK + 1)
+
+        w1_sorted = const.tile([P, GROUPS, PACK, P], BF16)
+        for g in range(GROUPS):
+            nc.vector.tensor_copy(
+                out=w1_sorted[:, g],
+                in_=w1_sb[:, g * K_PASS : (g + 1) * K_PASS].rearrange("l (p t) -> l t p", t=PACK),
+            )
+        b1 = const.tile([P, GROUPS, PACK], F32)
+        nc.vector.tensor_copy(out=b1[:], in_=b1_bf[:])
+
+        sum_xu = const.tile([P, TILES], F32)
+        sum_softplus = const.tile([P, TILES], F32)
+
+        zt_ps = {}
+        zT = {}
+        hd_ps = {}
+        planes = {}
+        grouped = {}
+        codes = {}
+        scales = {}
+        v_ps = {}
+        u_sb = {}
+
+        def transpose_z(k, ii):
+            if ii == 0:
+                bank = psum_t.tile([P, COLS], BF16, name="zt_ps")
+                zt_ps[k] = bank
+            i = k * BLOCK + ii
+            chunk = z_sb[k // Z_CHUNK]
+            nc.tensor.transpose(
+                zt_ps[k][:, ii * P : (ii + 1) * P], chunk[:, i % (Z_CHUNK * BLOCK), :], ident[:]
+            )
+
+        def copy_zT(k):
+            zT_block = work.tile([P, COLS], BF16, name="zT")
+            nc.vector.tensor_copy(out=zT_block[:], in_=zt_ps[k][:])
+            zT[k] = zT_block
+
+        def hidden_matmul(k, g, t):
+            bank = psum_h.tile([P, COLS], F32, name="hd_ps")
+            nc.tensor.matmul(out=bank[:], lhsT=w1_sorted[:, g, t, :], rhs=zT[k][:], start=True, stop=True)
+            hd_ps[(k, g, t)] = bank
+
+        def bias_relu(k, g, t):
+            if t == 0:
+                four = work.tile([P, PACK, COLS], BF16, name="planes")
+                planes[(k, g)] = four
+            dst = planes[(k, g)][:, t, :]
+            src = hd_ps[(k, g, t)]
+            if g == GROUPS - 1 and t == PACK - 1:
+                nc.vector.tensor_scalar(
+                    out=dst, in0=src[:], scalar1=b1[:, g, t : t + 1], scalar2=0.0, op0=ALU.add, op1=ALU.max
+                )
+            else:
+                nc.scalar.activation(out=dst, in_=src[:], func=ACT.Relu, bias=b1[:, g, t : t + 1], scale=1.0)
+
+        def regroup(k, g):
+            words = work.tile([P, COLS, PACK], BF16, name="grouped", align_bytes=64)
+            nc.vector.tensor_copy(
+                out=words[:].rearrange("p (c i) t -> p c t i", i=4),
+                in_=planes[(k, g)][:].rearrange("p t (c i) -> p c t i", i=4),
+            )
+            grouped[(k, g)] = words
+
+        def quantise(k, g):
+            packed = work.tile([P, COLS], U32, name="codes", bufs=4, align_bytes=64)
+            plane = work.tile([P, COLS], U8, name="scales", bufs=4, align_bytes=64)
+            nc.vector.quantize_mx(
+                out=packed[:].bitcast(FP8X4),
+                scales=plane[:],
+                in_=grouped[(k, g)][:].rearrange("p c t -> p (c t)"),
+            )
+            codes[(k, g)] = packed
+            scales[(k, g)] = plane
+
+        def output_matmul(k, ii):
+            bank = psum_v.tile([P, D], F32, name="v_ps")
+            rows = slice(ii * P, (ii + 1) * P)
+            for g in range(GROUPS):
+                nc.tensor.matmul_mx(
+                    out=bank[:],
+                    lhsT=codes[(k, g)][:, rows].bitcast(FP8X4),
+                    lhsT_scale=scales[(k, g)][:, rows],
+                    rhs=w2_words[:, g, :].bitcast(FP4X4),
+                    rhs_scale=w2_scales[:, g, :],
+                    start=(g == 0),
+                    stop=(g == GROUPS - 1),
+                )
+            v_ps[(k, ii)] = bank
+
+        def add_bias2(k, ii):
+            if ii == 0:
+                u_block = work.tile([P, BLOCK, D], F32, name="u", bufs=7)
+                u_sb[k] = u_block
+            nc.vector.tensor_tensor(out=u_sb[k][:, ii, :], in0=v_ps[(k, ii)][:], in1=b2_all[:], op=ALU.add)
+
+        def dot_with_x(k, ii):
+            product = work.tile([P, D], F32, name="product", bufs=2)
+            i = k * BLOCK + ii
+            nc.vector.scalar_tensor_tensor(
+                out=product[:],
+                in0=u_sb[k][:, ii, :],
+                scalar=1.0,
+                in1=x_sb[k][:, ii, :],
+                op0=ALU.mult,
+                op1=ALU.mult,
+                accum_out=sum_xu[:, i : i + 1],
+            )
+
+        def exponential(k, half):
+            pair = u_sb[k][:, 2 * half : 2 * half + 2, :]
+            nc.scalar.activation(out=pair, in_=pair, func=ACT.Exp)
+
+        def log1p_sum(k, ii):
+            i = k * BLOCK + ii
+            nc.scalar.activation(
+                out=u_sb[k][:, ii, :],
+                in_=u_sb[k][:, ii, :],
+                func=ACT.Ln,
+                bias=one[:, 0:1],
+                scale=1.0,
+                accum_out=sum_softplus[:, i : i + 1],
+            )
+
+        def real(k):
+            return 0 <= k < BLOCKS
+
+        for k in range(-2, BLOCKS + SUPER + 1):
+            turn = (k - SUPER - 1) % SUPER
+            first = ((k - SUPER - 1) // SUPER) * SUPER
+            for q in range(4):
+                if real(k - 2):
+                    output_matmul(k - 2, q)
+                if real(k):
+                    hidden_matmul(k, q // 2, 2 * (q % 2))
+                    hidden_matmul(k, q // 2, 2 * (q % 2) + 1)
+                if real(k + 2):
+                    transpose_z(k + 2, q)
+                if real(k):
+                    bias_relu(k, q // 2, 2 * (q % 2))
+                    bias_relu(k, q // 2, 2 * (q % 2) + 1)
+                if first >= 0:
+                    served = first + 2 * (turn % 2) + q // 2
+                    if turn < 2:
+                        exponential(served, q % 2)
+                    else:
+                        log1p_sum(served, 2 * (q % 2))
+                        log1p_sum(served, 2 * (q % 2) + 1)
+                if real(k - 2):
+                    add_bias2(k - 2, q)
+                if q == 0 and real(k - 1):
+                    regroup(k - 1, 1)
+                if q == 1 and real(k - 1):
+                    quantise(k - 1, 0)
+                if q == 2 and real(k):
+                    regroup(k, 0)
+                if q == 3 and real(k - 1):
+                    quantise(k - 1, 1)
+                if q == 3 and real(k + 2):
+                    copy_zT(k + 2)
+                if real(k - 2):
+                    dot_with_x(k - 2, q)
+
+        result = const.tile([P, TILES], F32)
+        nc.vector.tensor_sub(out=result[:], in0=sum_xu[:], in1=sum_softplus[:])
+        nc.sync.dma_start(out=out_rows, in_=result[:])

@@ -24,6 +24,9 @@ BLOCKS = TILES // BLOCK
 COLS = BLOCK * P
 Z_CHUNK = 4
 SUPER = 4
+LAG_OUT = 2
+LAG_EXP = LAG_OUT + SUPER - 1
+LAG_X = 6
 
 FLOPS = 2 * B * L * H + 2 * B * H * D
 
@@ -104,6 +107,7 @@ def tile_vae_pb_t_kernel(tc, z, x, Wd1, bd1, Wd2_words, Wd2_scales, bd2, out):
         scales = {}
         v_ps = {}
         u_sb = {}
+        e_sb = {}
 
         def transpose_z(k, ii):
             if ii == 0:
@@ -117,7 +121,7 @@ def tile_vae_pb_t_kernel(tc, z, x, Wd1, bd1, Wd2_words, Wd2_scales, bd2, out):
 
         def copy_zT(k):
             zT_block = work.tile([P, COLS], BF16, name="zT")
-            nc.vector.tensor_copy(out=zT_block[:], in_=zt_ps[k][:])
+            nc.scalar.copy(out=zT_block[:], in_=zt_ps[k][:])
             zT[k] = zT_block
 
         def hidden_matmul(k, g, t):
@@ -125,13 +129,13 @@ def tile_vae_pb_t_kernel(tc, z, x, Wd1, bd1, Wd2_words, Wd2_scales, bd2, out):
             nc.tensor.matmul(out=bank[:], lhsT=w1_sorted[:, g, t, :], rhs=zT[k][:], start=True, stop=True)
             hd_ps[(k, g, t)] = bank
 
-        def bias_relu(k, g, t):
+        def bias_relu(k, g, t, on_vector):
             if t == 0:
                 four = work.tile([P, PACK, COLS], BF16, name="planes")
                 planes[(k, g)] = four
             dst = planes[(k, g)][:, t, :]
             src = hd_ps[(k, g, t)]
-            if g == GROUPS - 1 and t == PACK - 1:
+            if on_vector:
                 nc.vector.tensor_scalar(
                     out=dst, in0=src[:], scalar1=b1[:, g, t : t + 1], scalar2=0.0, op0=ALU.add, op1=ALU.max
                 )
@@ -174,7 +178,7 @@ def tile_vae_pb_t_kernel(tc, z, x, Wd1, bd1, Wd2_words, Wd2_scales, bd2, out):
 
         def add_bias2(k, ii):
             if ii == 0:
-                u_block = work.tile([P, BLOCK, D], F32, name="u", bufs=7)
+                u_block = work.tile([P, BLOCK, D], F32, name="u", bufs=6)
                 u_sb[k] = u_block
             nc.vector.tensor_tensor(out=u_sb[k][:, ii, :], in0=v_ps[(k, ii)][:], in1=b2_all[:], op=ALU.add)
 
@@ -192,14 +196,17 @@ def tile_vae_pb_t_kernel(tc, z, x, Wd1, bd1, Wd2_words, Wd2_scales, bd2, out):
             )
 
         def exponential(k, half):
-            pair = u_sb[k][:, 2 * half : 2 * half + 2, :]
-            nc.scalar.activation(out=pair, in_=pair, func=ACT.Exp)
+            if half == 0:
+                e_block = work.tile([P, BLOCK, D], F32, name="e", bufs=SUPER)
+                e_sb[k] = e_block
+            pair = slice(2 * half, 2 * half + 2)
+            nc.scalar.activation(out=e_sb[k][:, pair, :], in_=u_sb[k][:, pair, :], func=ACT.Exp)
 
         def log1p_sum(k, ii):
             i = k * BLOCK + ii
             nc.scalar.activation(
-                out=u_sb[k][:, ii, :],
-                in_=u_sb[k][:, ii, :],
+                out=e_sb[k][:, ii, :],
+                in_=e_sb[k][:, ii, :],
                 func=ACT.Ln,
                 bias=one[:, 0:1],
                 scale=1.0,
@@ -209,29 +216,34 @@ def tile_vae_pb_t_kernel(tc, z, x, Wd1, bd1, Wd2_words, Wd2_scales, bd2, out):
         def real(k):
             return 0 <= k < BLOCKS
 
-        for k in range(-2, BLOCKS + SUPER + 1):
-            turn = (k - SUPER - 1) % SUPER
-            first = ((k - SUPER - 1) // SUPER) * SUPER
+        for k in range(-2, BLOCKS + LAG_X):
+            turn = (k - LAG_EXP) % SUPER
+            first = ((k - LAG_EXP) // SUPER) * SUPER
+            cycle_runs = 0 <= first < BLOCKS
             for q in range(4):
-                if real(k - 2):
-                    output_matmul(k - 2, q)
+                g = q // 2
+                t = 2 * (q % 2)
+                if real(k - LAG_OUT):
+                    output_matmul(k - LAG_OUT, q)
                 if real(k):
-                    hidden_matmul(k, q // 2, 2 * (q % 2))
-                    hidden_matmul(k, q // 2, 2 * (q % 2) + 1)
+                    hidden_matmul(k, g, t)
+                    hidden_matmul(k, g, t + 1)
                 if real(k + 2):
                     transpose_z(k + 2, q)
                 if real(k):
-                    bias_relu(k, q // 2, 2 * (q % 2))
-                    bias_relu(k, q // 2, 2 * (q % 2) + 1)
-                if first >= 0:
+                    bias_relu(k, g, t, False)
+                    bias_relu(k, g, t + 1, cycle_runs and t + 1 == PACK - 1)
+                if q == 3 and real(k + 2):
+                    copy_zT(k + 2)
+                if cycle_runs:
                     served = first + 2 * (turn % 2) + q // 2
                     if turn < 2:
                         exponential(served, q % 2)
                     else:
                         log1p_sum(served, 2 * (q % 2))
                         log1p_sum(served, 2 * (q % 2) + 1)
-                if real(k - 2):
-                    add_bias2(k - 2, q)
+                if real(k - LAG_OUT):
+                    add_bias2(k - LAG_OUT, q)
                 if q == 0 and real(k - 1):
                     regroup(k - 1, 1)
                 if q == 1 and real(k - 1):
@@ -240,10 +252,8 @@ def tile_vae_pb_t_kernel(tc, z, x, Wd1, bd1, Wd2_words, Wd2_scales, bd2, out):
                     regroup(k, 0)
                 if q == 3 and real(k - 1):
                     quantise(k - 1, 1)
-                if q == 3 and real(k + 2):
-                    copy_zT(k + 2)
-                if real(k - 2):
-                    dot_with_x(k - 2, q)
+                if real(k - LAG_X):
+                    dot_with_x(k - LAG_X, q)
 
         result = const.tile([P, TILES], F32)
         nc.vector.tensor_sub(out=result[:], in0=sum_xu[:], in1=sum_softplus[:])

@@ -41,8 +41,8 @@ def tile_vae_pb_t_kernel(tc, z, x, Wd1, bd1, Wd2_words, Wd2_scales, bd2, out):
         const = ctx.enter_context(tc.tile_pool(name="const", bufs=1))
         work = ctx.enter_context(tc.tile_pool(name="work", bufs=3))
         psum_t = ctx.enter_context(tc.psum_pool(name="psum_t", bufs=1))
-        psum_h = ctx.enter_context(tc.psum_pool(name="psum_h", bufs=4))
-        psum_v = ctx.enter_context(tc.psum_pool(name="psum_v", bufs=3))
+        psum_h = ctx.enter_context(tc.psum_pool(name="psum_h", bufs=5))
+        psum_v = ctx.enter_context(tc.psum_pool(name="psum_v", bufs=2))
         ctx.enter_context(tc.manual_schedule())
 
         w2_scales = const.tile([P, GROUPS, D], U8, align_bytes=64)
@@ -242,18 +242,15 @@ def tile_vae_pb_t_kernel(tc, z, x, Wd1, bd1, Wd2_words, Wd2_scales, bd2, out):
                     else:
                         log1p_sum(served, 2 * (q % 2))
                         log1p_sum(served, 2 * (q % 2) + 1)
-                if real(k - LAG_OUT):
-                    add_bias2(k - LAG_OUT, q)
-                if q == 0 and real(k - 1):
-                    regroup(k - 1, 1)
-                if q == 1 and real(k - 1):
-                    quantise(k - 1, 0)
-                if q == 2 and real(k):
-                    regroup(k, 0)
-                if q == 3 and real(k - 1):
-                    quantise(k - 1, 1)
+                if real(k - 1):
+                    if q < 2:
+                        regroup(k - 1, q)
+                    else:
+                        quantise(k - 1, q - 2)
                 if real(k - LAG_X):
                     dot_with_x(k - LAG_X, q)
+                if real(k - LAG_OUT):
+                    add_bias2(k - LAG_OUT, q)
 
         result = const.tile([P, TILES], F32)
         nc.vector.tensor_sub(out=result[:], in0=sum_xu[:], in1=sum_softplus[:])

@@ -144,10 +144,22 @@ def tile_vae_pb_t_kernel(tc, z, x, Wd1, bd1, Wd2_words, Wd2_scales, bd2, out):
 
         def regroup(k, g):
             words = work.tile([P, COLS, PACK], BF16, name="grouped", align_bytes=64)
-            nc.vector.tensor_copy(
-                out=words[:].rearrange("p (c i) t -> p c t i", i=4),
-                in_=planes[(k, g)][:].rearrange("p t (c i) -> p c t i", i=4),
-            )
+            if g == 0:
+                nc.vector.tensor_copy(
+                    out=words[:].rearrange("p (c i) t -> p c t i", i=4),
+                    in_=planes[(k, g)][:].rearrange("p t (c i) -> p c t i", i=4),
+                )
+            else:
+                for ii in range(BLOCK):
+                    rows = slice(ii * P, (ii + 1) * P)
+                    nc.gpsimd.tensor_scalar(
+                        out=words[:, rows, :],
+                        in0=planes[(k, g)][:, :, rows].rearrange("p t c -> p c t"),
+                        scalar1=1.0,
+                        scalar2=0.0,
+                        op0=ALU.mult,
+                        op1=ALU.add,
+                    )
             grouped[(k, g)] = words
 
         def quantise(k, g):
@@ -232,7 +244,7 @@ def tile_vae_pb_t_kernel(tc, z, x, Wd1, bd1, Wd2_words, Wd2_scales, bd2, out):
                     transpose_z(k + 2, q)
                 if real(k):
                     bias_relu(k, g, t, False)
-                    bias_relu(k, g, t + 1, cycle_runs and t + 1 == PACK - 1)
+                    bias_relu(k, g, t + 1, cycle_runs and q >= 1)
                 if q == 3 and real(k + 2):
                     copy_zT(k + 2)
                 if cycle_runs:

@@ -27,6 +27,14 @@ SUPER = 4
 LAG_OUT = 2
 LAG_EXP = LAG_OUT + SUPER - 1
 LAG_X = 6
+GA = 0
+U_BUFS = 6
+A_UNITS = 3
+A_BANKS = 3
+SUPERS = (4, 4, 4, 4)
+UNITS_A_ROUND = 4
+E_BUFS = 4
+GB = 1
 
 FLOPS = 2 * B * L * H + 2 * B * H * D
 
@@ -41,7 +49,8 @@ def tile_vae_pb_t_kernel(tc, z, x, Wd1, bd1, Wd2_words, Wd2_scales, bd2, out):
         const = ctx.enter_context(tc.tile_pool(name="const", bufs=1))
         work = ctx.enter_context(tc.tile_pool(name="work", bufs=3))
         psum_t = ctx.enter_context(tc.psum_pool(name="psum_t", bufs=1))
-        psum_h = ctx.enter_context(tc.psum_pool(name="psum_h", bufs=5))
+        psum_a = ctx.enter_context(tc.psum_pool(name="psum_a", bufs=A_BANKS))
+        psum_b = ctx.enter_context(tc.psum_pool(name="psum_b", bufs=5 - A_BANKS))
         psum_v = ctx.enter_context(tc.psum_pool(name="psum_v", bufs=2))
         ctx.enter_context(tc.manual_schedule())
 
@@ -71,6 +80,8 @@ def tile_vae_pb_t_kernel(tc, z, x, Wd1, bd1, Wd2_words, Wd2_scales, bd2, out):
         nc.sync.dma_start(out=w1_sb[:], in_=Wd1)
         b1_bf = const.tile([P, GROUPS, PACK], BF16)
         nc.sync.dma_start(out=b1_bf[:], in_=bd1.rearrange("(g p t) -> p g t", g=GROUPS, t=PACK))
+        b1_line = const.tile([P, K_PASS], BF16)
+        nc.sync.dma_start(out=b1_line[0:1, :], in_=bd1[GA * K_PASS : (GA + 1) * K_PASS].rearrange("(o k) -> o k", o=1))
         w2_words = const.tile([P, GROUPS, 2 * D], U8, align_bytes=64)
         for g in range(GROUPS):
             nc.sync.dma_start(out=w2_words[:, g, :].bitcast(I32), in_=Wd2_words[g].bitcast(I32))
@@ -98,9 +109,22 @@ def tile_vae_pb_t_kernel(tc, z, x, Wd1, bd1, Wd2_words, Wd2_scales, bd2, out):
         sum_xu = const.tile([P, TILES], F32)
         sum_softplus = const.tile([P, TILES], F32)
 
+        b1_rows = const.tile([P, P, PACK], F32)
+        zeros = const.tile([P, P], F32)
+        nc.vector.memset(zeros[:], 0.0)
+        for t in range(PACK):
+            nc.vector.tensor_scalar_add(out=b1_rows[:, :, t], in0=zeros[:], scalar1=b1[:, GA, t : t + 1])
+
+        bias_w = const.tile([P, PACK, P], BF16)
+        nc.vector.memset(bias_w[:], 0.0)
+        nc.vector.tensor_copy(out=bias_w[0:1], in_=b1_line[0:1, :].rearrange("o (p t) -> o t p", t=PACK))
+        ones_bf = const.tile([P, P], BF16)
+        nc.vector.memset(ones_bf[:], 1.0)
+
         zt_ps = {}
         zT = {}
-        hd_ps = {}
+        ha_ps = {}
+        hb_ps = {}
         planes = {}
         grouped = {}
         codes = {}
@@ -124,47 +148,70 @@ def tile_vae_pb_t_kernel(tc, z, x, Wd1, bd1, Wd2_words, Wd2_scales, bd2, out):
             nc.scalar.copy(out=zT_block[:], in_=zt_ps[k][:])
             zT[k] = zT_block
 
-        def hidden_matmul(k, g, t):
-            bank = psum_h.tile([P, COLS], F32, name="hd_ps")
-            nc.tensor.matmul(out=bank[:], lhsT=w1_sorted[:, g, t, :], rhs=zT[k][:], start=True, stop=True)
-            hd_ps[(k, g, t)] = bank
+        def hidden_a(k, ii):
+            bank = psum_a.tile([P, PACK, P], F32, name="ha_ps")
+            with_bias = ii >= a_units(k)
+            for t in range(PACK):
+                nc.tensor.matmul(
+                    out=bank[:, t, :], lhsT=w1_sorted[:, GA, t, :], rhs=zT[k][:, ii * P : (ii + 1) * P],
+                    start=True, stop=not with_bias,
+                )
+                if with_bias:
+                    nc.tensor.matmul(out=bank[:, t, :], lhsT=bias_w[:, t, :], rhs=ones_bf[:], start=False, stop=True)
+            ha_ps[(k, ii)] = bank
 
-        def bias_relu(k, g, t, on_vector):
+        def evacuate_c(k, ii):
+            nc.scalar.activation(
+                out=grouped[(k, GA)][:, ii * P : (ii + 1) * P, :],
+                in_=ha_ps[(k, ii)][:].rearrange("p t c -> p c t"),
+                func=ACT.Relu,
+            )
+
+        def evacuate_a(k, ii):
+            if ii == 0:
+                words = work.tile([P, COLS, PACK], BF16, name="grouped_a", bufs=2, align_bytes=64)
+                grouped[(k, GA)] = words
+            nc.vector.tensor_tensor(
+                out=grouped[(k, GA)][:, ii * P : (ii + 1) * P, :],
+                in0=ha_ps[(k, ii)][:].rearrange("p t c -> p c t"),
+                in1=b1_rows[:],
+                op=ALU.add,
+            )
+
+        def relu_a(k):
+            flat = grouped[(k, GA)][:, : a_units(k) * P, :].rearrange("p c t -> p (c t)")
+            nc.vector.tensor_scalar_max(out=flat, in0=flat, scalar1=0.0)
+
+        def hidden_b(k, t):
+            bank = psum_b.tile([P, COLS], F32, name="hb_ps")
+            nc.tensor.matmul(out=bank[:], lhsT=w1_sorted[:, GB, t, :], rhs=zT[k][:], start=True, stop=True)
+            hb_ps[(k, t)] = bank
+
+        def evacuate_b(k, t):
             if t == 0:
-                four = work.tile([P, PACK, COLS], BF16, name="planes")
-                planes[(k, g)] = four
-            dst = planes[(k, g)][:, t, :]
-            src = hd_ps[(k, g, t)]
-            if on_vector:
-                nc.vector.tensor_scalar(
-                    out=dst, in0=src[:], scalar1=b1[:, g, t : t + 1], scalar2=0.0, op0=ALU.add, op1=ALU.max
-                )
-            else:
-                nc.scalar.activation(out=dst, in_=src[:], func=ACT.Relu, bias=b1[:, g, t : t + 1], scale=1.0)
+                four = work.tile([P, PACK, COLS], BF16, name="planes", bufs=2)
+                planes[k] = four
+            nc.scalar.activation(
+                out=planes[k][:, t, :], in_=hb_ps[(k, t)][:], func=ACT.Relu, bias=b1[:, GB, t : t + 1], scale=1.0
+            )
 
-        def regroup(k, g):
-            words = work.tile([P, COLS, PACK], BF16, name="grouped", align_bytes=64)
-            if g == 0:
-                nc.vector.tensor_copy(
-                    out=words[:].rearrange("p (c i) t -> p c t i", i=4),
-                    in_=planes[(k, g)][:].rearrange("p t (c i) -> p c t i", i=4),
-                )
-            else:
-                for ii in range(BLOCK):
-                    rows = slice(ii * P, (ii + 1) * P)
-                    nc.gpsimd.tensor_scalar(
-                        out=words[:, rows, :],
-                        in0=planes[(k, g)][:, :, rows].rearrange("p t c -> p c t"),
-                        scalar1=1.0,
-                        scalar2=0.0,
-                        op0=ALU.mult,
-                        op1=ALU.add,
-                    )
-            grouped[(k, g)] = words
+        def regroup_b(k, ii):
+            if ii == 0:
+                words = work.tile([P, COLS, PACK], BF16, name="grouped_b", bufs=1, align_bytes=64)
+                grouped[(k, GB)] = words
+            rows = slice(ii * P, (ii + 1) * P)
+            nc.gpsimd.tensor_scalar(
+                out=grouped[(k, GB)][:, rows, :],
+                in0=planes[k][:, :, rows].rearrange("p t c -> p c t"),
+                scalar1=1.0,
+                scalar2=0.0,
+                op0=ALU.mult,
+                op1=ALU.add,
+            )
 
         def quantise(k, g):
-            packed = work.tile([P, COLS], U32, name="codes", bufs=4, align_bytes=64)
-            plane = work.tile([P, COLS], U8, name="scales", bufs=4, align_bytes=64)
+            packed = work.tile([P, COLS], U32, name="codes%d" % g, bufs=3, align_bytes=64)
+            plane = work.tile([P, COLS], U8, name="scales%d" % g, bufs=3, align_bytes=64)
             nc.vector.quantize_mx(
                 out=packed[:].bitcast(FP8X4),
                 scales=plane[:],
@@ -190,7 +237,7 @@ def tile_vae_pb_t_kernel(tc, z, x, Wd1, bd1, Wd2_words, Wd2_scales, bd2, out):
 
         def add_bias2(k, ii):
             if ii == 0:
-                u_block = work.tile([P, BLOCK, D], F32, name="u", bufs=6)
+                u_block = work.tile([P, BLOCK, D], F32, name="u", bufs=U_BUFS)
                 u_sb[k] = u_block
             nc.vector.tensor_tensor(out=u_sb[k][:, ii, :], in0=v_ps[(k, ii)][:], in1=b2_all[:], op=ALU.add)
 
@@ -209,7 +256,7 @@ def tile_vae_pb_t_kernel(tc, z, x, Wd1, bd1, Wd2_words, Wd2_scales, bd2, out):
 
         def exponential(k, half):
             if half == 0:
-                e_block = work.tile([P, BLOCK, D], F32, name="e", bufs=SUPER)
+                e_block = work.tile([P, BLOCK, D], F32, name="e", bufs=E_BUFS)
                 e_sb[k] = e_block
             pair = slice(2 * half, 2 * half + 2)
             nc.scalar.activation(out=e_sb[k][:, pair, :], in_=u_sb[k][:, pair, :], func=ACT.Exp)
@@ -228,41 +275,72 @@ def tile_vae_pb_t_kernel(tc, z, x, Wd1, bd1, Wd2_words, Wd2_scales, bd2, out):
         def real(k):
             return 0 <= k < BLOCKS
 
+        def a_units(k):
+            return A_UNITS
+
+        units = []
+        first = 0
+        for size in SUPERS:
+            for b in range(first, first + size):
+                units.extend([("exp", b, 0), ("exp", b, 1)])
+            for b in range(first, first + size):
+                units.extend([("ln", b, 0), ("ln", b, 1)])
+            first += size
+
+        taken = 0
         for k in range(-2, BLOCKS + LAG_X):
-            turn = (k - LAG_EXP) % SUPER
-            first = ((k - LAG_EXP) // SUPER) * SUPER
-            cycle_runs = 0 <= first < BLOCKS
+            ko = k - LAG_OUT
             for q in range(4):
-                g = q // 2
-                t = 2 * (q % 2)
-                if real(k - LAG_OUT):
-                    output_matmul(k - LAG_OUT, q)
-                if real(k):
-                    hidden_matmul(k, g, t)
-                    hidden_matmul(k, g, t + 1)
-                if real(k + 2):
-                    transpose_z(k + 2, q)
-                if real(k):
-                    bias_relu(k, g, t, False)
-                    bias_relu(k, g, t + 1, cycle_runs and q >= 1)
-                if q == 3 and real(k + 2):
-                    copy_zT(k + 2)
-                if cycle_runs:
-                    served = first + 2 * (turn % 2) + q // 2
-                    if turn < 2:
-                        exponential(served, q % 2)
-                    else:
-                        log1p_sum(served, 2 * (q % 2))
-                        log1p_sum(served, 2 * (q % 2) + 1)
                 if real(k - 1):
-                    if q < 2:
-                        regroup(k - 1, q)
+                    regroup_b(k - 1, q)
+            for q in range(UNITS_A_ROUND):
+                if taken < len(units) and units[taken][1] < ko:
+                    kind, b, half = units[taken]
+                    taken += 1
+                    if kind == "exp":
+                        exponential(b, half)
                     else:
-                        quantise(k - 1, q - 2)
+                        log1p_sum(b, 2 * half)
+                        log1p_sum(b, 2 * half + 1)
+            if real(ko):
+                output_matmul(ko, 0)
+                output_matmul(ko, 1)
+            if real(k):
+                for q in range(a_units(k)):
+                    evacuate_a(k, q)
+                    if q + A_BANKS < BLOCK:
+                        hidden_a(k, q + A_BANKS)
+            if real(ko):
+                for q in range(4):
+                    add_bias2(ko, q)
+                    if q + 2 < BLOCK:
+                        output_matmul(ko, q + 2)
+            if real(k):
+                relu_a(k)
+                for q in range(a_units(k), BLOCK):
+                    evacuate_c(k, q)
+                    if q + A_BANKS < BLOCK:
+                        hidden_a(k, q + A_BANKS)
+            if real(k + 1):
+                for q in range(A_BANKS - 1):
+                    hidden_a(k + 1, q)
+            for q in range(4):
                 if real(k - LAG_X):
                     dot_with_x(k - LAG_X, q)
-                if real(k - LAG_OUT):
-                    add_bias2(k - LAG_OUT, q)
+            if real(k - 1):
+                quantise(k - 1, GA)
+                quantise(k - 1, GB)
+            for t in range(PACK):
+                if real(k):
+                    hidden_b(k, t)
+                    evacuate_b(k, t)
+            if real(k + 2):
+                for q in range(4):
+                    transpose_z(k + 2, q)
+                copy_zT(k + 2)
+            if real(k + 1):
+                hidden_a(k + 1, A_BANKS - 1)
+        assert taken == len(units)
 
         result = const.tile([P, TILES], F32)
         nc.vector.tensor_sub(out=result[:], in0=sum_xu[:], in1=sum_softplus[:])

@@ -34,6 +34,7 @@ A_BANKS = 3
 SUPERS = (4, 4, 4, 4)
 UNITS_A_ROUND = 4
 E_BUFS = 4
+EARLY = 3
 GB = 1
 
 FLOPS = 2 * B * L * H + 2 * B * H * D
@@ -126,6 +127,7 @@ def tile_vae_pb_t_kernel(tc, z, x, Wd1, bd1, Wd2_words, Wd2_scales, bd2, out):
         ha_ps = {}
         hb_ps = {}
         planes = {}
+        planes_a = {}
         grouped = {}
         codes = {}
         scales = {}
@@ -169,7 +171,7 @@ def tile_vae_pb_t_kernel(tc, z, x, Wd1, bd1, Wd2_words, Wd2_scales, bd2, out):
 
         def evacuate_a(k, ii):
             if ii == 0:
-                words = work.tile([P, COLS, PACK], BF16, name="grouped_a", bufs=2, align_bytes=64)
+                words = work.tile([P, COLS, PACK], BF16, name="grouped_a", bufs=3, align_bytes=64)
                 grouped[(k, GA)] = words
             nc.vector.tensor_tensor(
                 out=grouped[(k, GA)][:, ii * P : (ii + 1) * P, :],
@@ -195,14 +197,33 @@ def tile_vae_pb_t_kernel(tc, z, x, Wd1, bd1, Wd2_words, Wd2_scales, bd2, out):
                 out=planes[k][:, t, :], in_=hb_ps[(k, t)][:], func=ACT.Relu, bias=b1[:, GB, t : t + 1], scale=1.0
             )
 
-        def regroup_b(k, ii):
-            if ii == 0:
-                words = work.tile([P, COLS, PACK], BF16, name="grouped_b", bufs=1, align_bytes=64)
-                grouped[(k, GB)] = words
-            rows = slice(ii * P, (ii + 1) * P)
+        def hidden_early(k, t):
+            bank = psum_a.tile([P, COLS], F32, name="ha_ps")
+            nc.tensor.matmul(out=bank[:], lhsT=w1_sorted[:, GA, t, :], rhs=zT[k][:], start=True, stop=True)
+            ha_ps[(k, t)] = bank
+
+        def evacuate_early(k, t):
+            if t == 0:
+                four = work.tile([P, PACK, COLS], BF16, name="planes_a", bufs=2)
+                planes_a[k] = four
+            nc.scalar.activation(
+                out=planes_a[k][:, t, :], in_=ha_ps[(k, t)][:], func=ACT.Relu, bias=b1[:, GA, t : t + 1], scale=1.0
+            )
+
+        def regroup_early(k):
+            words = work.tile([P, COLS, PACK], BF16, name="grouped_a", bufs=3, align_bytes=64)
+            grouped[(k, GA)] = words
+            nc.vector.tensor_copy(
+                out=words[:].rearrange("p (c i) t -> p c t i", i=4),
+                in_=planes_a[k][:].rearrange("p t (c i) -> p c t i", i=4),
+            )
+
+        def regroup_b(k):
+            words = work.tile([P, COLS, PACK], BF16, name="grouped_b", bufs=1, align_bytes=64)
+            grouped[(k, GB)] = words
             nc.gpsimd.tensor_scalar(
-                out=grouped[(k, GB)][:, rows, :],
-                in0=planes[k][:, :, rows].rearrange("p t c -> p c t"),
+                out=words[:],
+                in0=planes[k][:].rearrange("p t c -> p c t"),
                 scalar1=1.0,
                 scalar2=0.0,
                 op0=ALU.mult,
@@ -278,6 +299,9 @@ def tile_vae_pb_t_kernel(tc, z, x, Wd1, bd1, Wd2_words, Wd2_scales, bd2, out):
         def a_units(k):
             return A_UNITS
 
+        def early(k):
+            return k < EARLY
+
         units = []
         first = 0
         for size in SUPERS:
@@ -290,9 +314,8 @@ def tile_vae_pb_t_kernel(tc, z, x, Wd1, bd1, Wd2_words, Wd2_scales, bd2, out):
         taken = 0
         for k in range(-2, BLOCKS + LAG_X):
             ko = k - LAG_OUT
-            for q in range(4):
-                if real(k - 1):
-                    regroup_b(k - 1, q)
+            if real(k - 1):
+                regroup_b(k - 1)
             for q in range(UNITS_A_ROUND):
                 if taken < len(units) and units[taken][1] < ko:
                     kind, b, half = units[taken]
@@ -305,25 +328,26 @@ def tile_vae_pb_t_kernel(tc, z, x, Wd1, bd1, Wd2_words, Wd2_scales, bd2, out):
             if real(ko):
                 output_matmul(ko, 0)
                 output_matmul(ko, 1)
-            if real(k):
+            if real(k) and not early(k):
                 for q in range(a_units(k)):
                     evacuate_a(k, q)
-                    if q + A_BANKS < BLOCK:
-                        hidden_a(k, q + A_BANKS)
             if real(ko):
                 for q in range(4):
                     add_bias2(ko, q)
                     if q + 2 < BLOCK:
                         output_matmul(ko, q + 2)
-            if real(k):
+            if real(k) and not early(k):
+                for q in range(A_BANKS, BLOCK):
+                    hidden_a(k, q)
+            if real(k) and not early(k):
                 relu_a(k)
                 for q in range(a_units(k), BLOCK):
                     evacuate_c(k, q)
-                    if q + A_BANKS < BLOCK:
-                        hidden_a(k, q + A_BANKS)
-            if real(k + 1):
+            if real(k + 1) and not early(k):
                 for q in range(A_BANKS - 1):
                     hidden_a(k + 1, q)
+            if real(k - 1) and early(k - 1):
+                regroup_early(k - 1)
             for q in range(4):
                 if real(k - LAG_X):
                     dot_with_x(k - LAG_X, q)
@@ -332,14 +356,18 @@ def tile_vae_pb_t_kernel(tc, z, x, Wd1, bd1, Wd2_words, Wd2_scales, bd2, out):
                 quantise(k - 1, GB)
             for t in range(PACK):
                 if real(k):
+                    if early(k):
+                        hidden_early(k, t)
+                        evacuate_early(k, t)
                     hidden_b(k, t)
                     evacuate_b(k, t)
             if real(k + 2):
                 for q in range(4):
                     transpose_z(k + 2, q)
                 copy_zT(k + 2)
-            if real(k + 1):
-                hidden_a(k + 1, A_BANKS - 1)
+            if real(k + 1) and not early(k + 1):
+                for q in range(A_BANKS - 1 if not early(k) else 0, A_BANKS):
+                    hidden_a(k + 1, q)
         assert taken == len(units)
 
         result = const.tile([P, TILES], F32)

@@ -26,15 +26,17 @@ Z_CHUNK = 4
 SUPER = 4
 LAG_OUT = 2
 LAG_EXP = LAG_OUT + SUPER - 1
-LAG_X = 6
 GA = 0
-U_BUFS = 6
-A_UNITS = 3
+U_BUFS = 9
 A_BANKS = 3
 SUPERS = (4, 4, 4, 4)
 UNITS_A_ROUND = 4
 E_BUFS = 4
-EARLY = 3
+EARLY = 5
+X_BUFS = 4
+DOTS_A_ROUND = 3
+DOTS_AT_THE_END = 8
+DRAIN = 8
 GB = 1
 
 FLOPS = 2 * B * L * H + 2 * B * H * D
@@ -72,7 +74,7 @@ def tile_vae_pb_t_kernel(tc, z, x, Wd1, bd1, Wd2_words, Wd2_scales, bd2, out):
             z_sb[c] = z_chunk
 
         def load_x(k):
-            x_block = const.tile([P, BLOCK, D], BF16, name="x%d" % k)
+            x_block = work.tile([P, BLOCK, D], BF16, name="x", bufs=X_BUFS)
             nc.sync.dma_start(out=x_block[:], in_=x_rows[:, k * BLOCK : (k + 1) * BLOCK, :])
             x_sb[k] = x_block
 
@@ -81,8 +83,6 @@ def tile_vae_pb_t_kernel(tc, z, x, Wd1, bd1, Wd2_words, Wd2_scales, bd2, out):
         nc.sync.dma_start(out=w1_sb[:], in_=Wd1)
         b1_bf = const.tile([P, GROUPS, PACK], BF16)
         nc.sync.dma_start(out=b1_bf[:], in_=bd1.rearrange("(g p t) -> p g t", g=GROUPS, t=PACK))
-        b1_line = const.tile([P, K_PASS], BF16)
-        nc.sync.dma_start(out=b1_line[0:1, :], in_=bd1[GA * K_PASS : (GA + 1) * K_PASS].rearrange("(o k) -> o k", o=1))
         w2_words = const.tile([P, GROUPS, 2 * D], U8, align_bytes=64)
         for g in range(GROUPS):
             nc.sync.dma_start(out=w2_words[:, g, :].bitcast(I32), in_=Wd2_words[g].bitcast(I32))
@@ -93,10 +93,10 @@ def tile_vae_pb_t_kernel(tc, z, x, Wd1, bd1, Wd2_words, Wd2_scales, bd2, out):
             )
         b2_all = const.tile([P, D], BF16)
         nc.sync.dma_start(out=b2_all[:], in_=bd2.partition_broadcast(P))
-        for k in range(BLOCKS):
+        for c in range(1, BLOCKS // Z_CHUNK):
+            load_z(c)
+        for k in range(X_BUFS):
             load_x(k)
-            if k % Z_CHUNK == 1 and k // Z_CHUNK + 1 < BLOCKS // Z_CHUNK:
-                load_z(k // Z_CHUNK + 1)
 
         w1_sorted = const.tile([P, GROUPS, PACK, P], BF16)
         for g in range(GROUPS):
@@ -115,12 +115,6 @@ def tile_vae_pb_t_kernel(tc, z, x, Wd1, bd1, Wd2_words, Wd2_scales, bd2, out):
         nc.vector.memset(zeros[:], 0.0)
         for t in range(PACK):
             nc.vector.tensor_scalar_add(out=b1_rows[:, :, t], in0=zeros[:], scalar1=b1[:, GA, t : t + 1])
-
-        bias_w = const.tile([P, PACK, P], BF16)
-        nc.vector.memset(bias_w[:], 0.0)
-        nc.vector.tensor_copy(out=bias_w[0:1], in_=b1_line[0:1, :].rearrange("o (p t) -> o t p", t=PACK))
-        ones_bf = const.tile([P, P], BF16)
-        nc.vector.memset(ones_bf[:], 1.0)
 
         zt_ps = {}
         zT = {}
@@ -152,22 +146,12 @@ def tile_vae_pb_t_kernel(tc, z, x, Wd1, bd1, Wd2_words, Wd2_scales, bd2, out):
 
         def hidden_a(k, ii):
             bank = psum_a.tile([P, PACK, P], F32, name="ha_ps")
-            with_bias = ii >= a_units(k)
             for t in range(PACK):
                 nc.tensor.matmul(
                     out=bank[:, t, :], lhsT=w1_sorted[:, GA, t, :], rhs=zT[k][:, ii * P : (ii + 1) * P],
-                    start=True, stop=not with_bias,
+                    start=True, stop=True,
                 )
-                if with_bias:
-                    nc.tensor.matmul(out=bank[:, t, :], lhsT=bias_w[:, t, :], rhs=ones_bf[:], start=False, stop=True)
             ha_ps[(k, ii)] = bank
-
-        def evacuate_c(k, ii):
-            nc.scalar.activation(
-                out=grouped[(k, GA)][:, ii * P : (ii + 1) * P, :],
-                in_=ha_ps[(k, ii)][:].rearrange("p t c -> p c t"),
-                func=ACT.Relu,
-            )
 
         def evacuate_a(k, ii):
             if ii == 0:
@@ -181,7 +165,7 @@ def tile_vae_pb_t_kernel(tc, z, x, Wd1, bd1, Wd2_words, Wd2_scales, bd2, out):
             )
 
         def relu_a(k):
-            flat = grouped[(k, GA)][:, : a_units(k) * P, :].rearrange("p c t -> p (c t)")
+            flat = grouped[(k, GA)][:].rearrange("p c t -> p (c t)")
             nc.vector.tensor_scalar_max(out=flat, in0=flat, scalar1=0.0)
 
         def hidden_b(k, t):
@@ -296,9 +280,6 @@ def tile_vae_pb_t_kernel(tc, z, x, Wd1, bd1, Wd2_words, Wd2_scales, bd2, out):
         def real(k):
             return 0 <= k < BLOCKS
 
-        def a_units(k):
-            return A_UNITS
-
         def early(k):
             return k < EARLY
 
@@ -312,8 +293,10 @@ def tile_vae_pb_t_kernel(tc, z, x, Wd1, bd1, Wd2_words, Wd2_scales, bd2, out):
             first += size
 
         taken = 0
-        for k in range(-2, BLOCKS + LAG_X):
+        dotted = 0
+        for k in range(-2, BLOCKS + DRAIN):
             ko = k - LAG_OUT
+            late = real(k) and not early(k)
             if real(k - 1):
                 regroup_b(k - 1)
             for q in range(UNITS_A_ROUND):
@@ -328,29 +311,34 @@ def tile_vae_pb_t_kernel(tc, z, x, Wd1, bd1, Wd2_words, Wd2_scales, bd2, out):
             if real(ko):
                 output_matmul(ko, 0)
                 output_matmul(ko, 1)
-            if real(k) and not early(k):
-                for q in range(a_units(k)):
-                    evacuate_a(k, q)
+            if late:
+                evacuate_a(k, 0)
+                hidden_a(k, 3)
+                evacuate_a(k, 1)
+                evacuate_a(k, 2)
             if real(ko):
-                for q in range(4):
-                    add_bias2(ko, q)
-                    if q + 2 < BLOCK:
-                        output_matmul(ko, q + 2)
-            if real(k) and not early(k):
-                for q in range(A_BANKS, BLOCK):
-                    hidden_a(k, q)
-            if real(k) and not early(k):
+                add_bias2(ko, 0)
+                output_matmul(ko, 2)
+                add_bias2(ko, 1)
+                output_matmul(ko, 3)
+            if late:
+                evacuate_a(k, 3)
+            if real(ko):
+                add_bias2(ko, 2)
+                add_bias2(ko, 3)
+            if late:
                 relu_a(k)
-                for q in range(a_units(k), BLOCK):
-                    evacuate_c(k, q)
             if real(k + 1) and not early(k):
                 for q in range(A_BANKS - 1):
                     hidden_a(k + 1, q)
             if real(k - 1) and early(k - 1):
                 regroup_early(k - 1)
-            for q in range(4):
-                if real(k - LAG_X):
-                    dot_with_x(k - LAG_X, q)
+            for q in range(DOTS_A_ROUND if real(k) else DOTS_AT_THE_END):
+                if dotted < TILES and dotted // BLOCK <= ko:
+                    dot_with_x(dotted // BLOCK, dotted % BLOCK)
+                    dotted += 1
+                    if dotted % BLOCK == 0 and dotted // BLOCK - 1 + X_BUFS < BLOCKS:
+                        load_x(dotted // BLOCK - 1 + X_BUFS)
             if real(k - 1):
                 quantise(k - 1, GA)
                 quantise(k - 1, GB)
@@ -368,7 +356,7 @@ def tile_vae_pb_t_kernel(tc, z, x, Wd1, bd1, Wd2_words, Wd2_scales, bd2, out):
             if real(k + 1) and not early(k + 1):
                 for q in range(A_BANKS - 1 if not early(k) else 0, A_BANKS):
                     hidden_a(k + 1, q)
-        assert taken == len(units)
+        assert taken == len(units) and dotted == TILES
 
         result = const.tile([P, TILES], F32)
         nc.vector.tensor_sub(out=result[:], in0=sum_xu[:], in1=sum_softplus[:])

@@ -29,14 +29,15 @@ LAG_EXP = LAG_OUT + SUPER - 1
 GA = 0
 U_BUFS = 9
 A_BANKS = 3
-SUPERS = (4, 4, 4, 4)
+SUPERS = (6, 6, 4)
 UNITS_A_ROUND = 4
-E_BUFS = 4
+E_BUFS = 6
 EARLY = 5
 X_BUFS = 4
 DOTS_A_ROUND = 3
 DOTS_AT_THE_END = 8
 DRAIN = 8
+BIASED = 7
 GB = 1
 
 FLOPS = 2 * B * L * H + 2 * B * H * D
@@ -67,22 +68,25 @@ def tile_vae_pb_t_kernel(tc, z, x, Wd1, bd1, Wd2_words, Wd2_scales, bd2, out):
         z_sb = {}
         x_sb = {}
 
-        def load_z(c):
-            z_chunk = const.tile([P, Z_CHUNK * BLOCK, L], BF16, name="z%d" % c)
-            first = c * Z_CHUNK * BLOCK
-            nc.sync.dma_start(out=z_chunk[:], in_=z_rows[:, first : first + Z_CHUNK * BLOCK, :])
-            z_sb[c] = z_chunk
+        def load_z(first, blocks):
+            z_chunk = const.tile([P, blocks * BLOCK, L], BF16, name="z%d" % first)
+            nc.sync.dma_start(out=z_chunk[:], in_=z_rows[:, first * BLOCK : (first + blocks) * BLOCK, :])
+            for k in range(first, first + blocks):
+                z_sb[k] = z_chunk[:, (k - first) * BLOCK : (k - first + 1) * BLOCK, :]
 
         def load_x(k):
             x_block = work.tile([P, BLOCK, D], BF16, name="x", bufs=X_BUFS)
             nc.sync.dma_start(out=x_block[:], in_=x_rows[:, k * BLOCK : (k + 1) * BLOCK, :])
             x_sb[k] = x_block
 
-        load_z(0)
+        load_z(0, 1)
         w1_sb = const.tile([P, H], BF16)
         nc.sync.dma_start(out=w1_sb[:], in_=Wd1)
         b1_bf = const.tile([P, GROUPS, PACK], BF16)
         nc.sync.dma_start(out=b1_bf[:], in_=bd1.rearrange("(g p t) -> p g t", g=GROUPS, t=PACK))
+        load_z(1, Z_CHUNK - 1)
+        b1_line = const.tile([P, K_PASS], BF16)
+        nc.sync.dma_start(out=b1_line[0:1, :], in_=bd1[GA * K_PASS : (GA + 1) * K_PASS].rearrange("(o k) -> o k", o=1))
         w2_words = const.tile([P, GROUPS, 2 * D], U8, align_bytes=64)
         for g in range(GROUPS):
             nc.sync.dma_start(out=w2_words[:, g, :].bitcast(I32), in_=Wd2_words[g].bitcast(I32))
@@ -94,8 +98,9 @@ def tile_vae_pb_t_kernel(tc, z, x, Wd1, bd1, Wd2_words, Wd2_scales, bd2, out):
         b2_all = const.tile([P, D], BF16)
         nc.sync.dma_start(out=b2_all[:], in_=bd2.partition_broadcast(P))
         for c in range(1, BLOCKS // Z_CHUNK):
-            load_z(c)
-        for k in range(X_BUFS):
+            load_x(c - 1)
+            load_z(c * Z_CHUNK, Z_CHUNK)
+        for k in range(BLOCKS // Z_CHUNK - 1, X_BUFS):
             load_x(k)
 
         w1_sorted = const.tile([P, GROUPS, PACK, P], BF16)
@@ -116,6 +121,12 @@ def tile_vae_pb_t_kernel(tc, z, x, Wd1, bd1, Wd2_words, Wd2_scales, bd2, out):
         for t in range(PACK):
             nc.vector.tensor_scalar_add(out=b1_rows[:, :, t], in0=zeros[:], scalar1=b1[:, GA, t : t + 1])
 
+        bias_w = const.tile([P, PACK, P], BF16)
+        nc.vector.memset(bias_w[:], 0.0)
+        nc.vector.tensor_copy(out=bias_w[0:1], in_=b1_line[0:1, :].rearrange("o (p t) -> o t p", t=PACK))
+        ones_bf = const.tile([P, P], BF16)
+        nc.vector.memset(ones_bf[:], 1.0)
+
         zt_ps = {}
         zT = {}
         ha_ps = {}
@@ -133,11 +144,7 @@ def tile_vae_pb_t_kernel(tc, z, x, Wd1, bd1, Wd2_words, Wd2_scales, bd2, out):
             if ii == 0:
                 bank = psum_t.tile([P, COLS], BF16, name="zt_ps")
                 zt_ps[k] = bank
-            i = k * BLOCK + ii
-            chunk = z_sb[k // Z_CHUNK]
-            nc.tensor.transpose(
-                zt_ps[k][:, ii * P : (ii + 1) * P], chunk[:, i % (Z_CHUNK * BLOCK), :], ident[:]
-            )
+            nc.tensor.transpose(zt_ps[k][:, ii * P : (ii + 1) * P], z_sb[k][:, ii, :], ident[:])
 
         def copy_zT(k):
             zT_block = work.tile([P, COLS], BF16, name="zT")
@@ -149,20 +156,29 @@ def tile_vae_pb_t_kernel(tc, z, x, Wd1, bd1, Wd2_words, Wd2_scales, bd2, out):
             for t in range(PACK):
                 nc.tensor.matmul(
                     out=bank[:, t, :], lhsT=w1_sorted[:, GA, t, :], rhs=zT[k][:, ii * P : (ii + 1) * P],
-                    start=True, stop=True,
+                    start=True, stop=not biased(k),
                 )
+                if biased(k):
+                    nc.tensor.matmul(out=bank[:, t, :], lhsT=bias_w[:, t, :], rhs=ones_bf[:], start=False, stop=True)
             ha_ps[(k, ii)] = bank
 
         def evacuate_a(k, ii):
             if ii == 0:
                 words = work.tile([P, COLS, PACK], BF16, name="grouped_a", bufs=3, align_bytes=64)
                 grouped[(k, GA)] = words
-            nc.vector.tensor_tensor(
-                out=grouped[(k, GA)][:, ii * P : (ii + 1) * P, :],
-                in0=ha_ps[(k, ii)][:].rearrange("p t c -> p c t"),
-                in1=b1_rows[:],
-                op=ALU.add,
-            )
+            if biased(k):
+                nc.vector.tensor_scalar_max(
+                    out=grouped[(k, GA)][:, ii * P : (ii + 1) * P, :],
+                    in0=ha_ps[(k, ii)][:].rearrange("p t c -> p c t"),
+                    scalar1=0.0,
+                )
+            else:
+                nc.vector.tensor_tensor(
+                    out=grouped[(k, GA)][:, ii * P : (ii + 1) * P, :],
+                    in0=ha_ps[(k, ii)][:].rearrange("p t c -> p c t"),
+                    in1=b1_rows[:],
+                    op=ALU.add,
+                )
 
         def relu_a(k):
             flat = grouped[(k, GA)][:].rearrange("p c t -> p (c t)")
@@ -283,6 +299,9 @@ def tile_vae_pb_t_kernel(tc, z, x, Wd1, bd1, Wd2_words, Wd2_scales, bd2, out):
         def early(k):
             return k < EARLY
 
+        def biased(k):
+            return k >= BLOCKS - BIASED
+
         units = []
         first = 0
         for size in SUPERS:
@@ -326,7 +345,7 @@ def tile_vae_pb_t_kernel(tc, z, x, Wd1, bd1, Wd2_words, Wd2_scales, bd2, out):
             if real(ko):
                 add_bias2(ko, 2)
                 add_bias2(ko, 3)
-            if late:
+            if late and not biased(k):
                 relu_a(k)
             if real(k + 1) and not early(k):
                 for q in range(A_BANKS - 1):
@@ -349,10 +368,11 @@ def tile_vae_pb_t_kernel(tc, z, x, Wd1, bd1, Wd2_words, Wd2_scales, bd2, out):
                         evacuate_early(k, t)
                     hidden_b(k, t)
                     evacuate_b(k, t)
-            if real(k + 2):
-                for q in range(4):
-                    transpose_z(k + 2, q)
-                copy_zT(k + 2)
+            for kz in (k + 2,) if k != -1 and k != 0 else (1, 2) if k == 0 else ():
+                if real(kz):
+                    for q in range(4):
+                        transpose_z(kz, q)
+                    copy_zT(kz)
             if real(k + 1) and not early(k + 1):
                 for q in range(A_BANKS - 1 if not early(k) else 0, A_BANKS):
                     hidden_a(k + 1, q)

@@ -29,9 +29,9 @@ LAG_EXP = LAG_OUT + SUPER - 1
 GA = 0
 U_BUFS = 9
 A_BANKS = 3
-SUPERS = (6, 6, 4)
+SUPERS = (4, 4, 4, 4)
 UNITS_A_ROUND = 4
-E_BUFS = 6
+E_BUFS = 4
 EARLY = 5
 X_BUFS = 4
 DOTS_A_ROUND = 3

@@ -146,9 +146,12 @@ def tile_vae_pb_t_kernel(tc, z, x, Wd1, bd1, Wd2_words, Wd2_scales, bd2, out):
                 zt_ps[k] = bank
             nc.tensor.transpose(zt_ps[k][:, ii * P : (ii + 1) * P], z_sb[k][:, ii, :], ident[:])
 
-        def copy_zT(k):
+        def copy_zT(k, on_vector):
             zT_block = work.tile([P, COLS], BF16, name="zT")
-            nc.scalar.copy(out=zT_block[:], in_=zt_ps[k][:])
+            if on_vector:
+                nc.vector.tensor_copy(out=zT_block[:], in_=zt_ps[k][:])
+            else:
+                nc.scalar.copy(out=zT_block[:], in_=zt_ps[k][:])
             zT[k] = zT_block
 
         def hidden_a(k, ii):
@@ -361,6 +364,10 @@ def tile_vae_pb_t_kernel(tc, z, x, Wd1, bd1, Wd2_words, Wd2_scales, bd2, out):
             if real(k - 1):
                 quantise(k - 1, GA)
                 quantise(k - 1, GB)
+            if biased(k) and real(k + 2):
+                for q in range(4):
+                    transpose_z(k + 2, q)
+                copy_zT(k + 2, True)
             for t in range(PACK):
                 if real(k):
                     if early(k):
@@ -369,10 +376,10 @@ def tile_vae_pb_t_kernel(tc, z, x, Wd1, bd1, Wd2_words, Wd2_scales, bd2, out):
                     hidden_b(k, t)
                     evacuate_b(k, t)
             for kz in (k + 2,) if k != -1 and k != 0 else (1, 2) if k == 0 else ():
-                if real(kz):
+                if real(kz) and not biased(k):
                     for q in range(4):
                         transpose_z(kz, q)
-                    copy_zT(kz)
+                    copy_zT(kz, False)
             if real(k + 1) and not early(k + 1):
                 for q in range(A_BANKS - 1 if not early(k) else 0, A_BANKS):
                     hidden_a(k + 1, q)

@@ -52,9 +52,8 @@ def tile_vae_pb_t_kernel(tc, z, x, Wd1, bd1, Wd2_words, Wd2_scales, bd2, out):
     with ExitStack() as ctx:
         const = ctx.enter_context(tc.tile_pool(name="const", bufs=1))
         work = ctx.enter_context(tc.tile_pool(name="work", bufs=3))
-        psum_t = ctx.enter_context(tc.psum_pool(name="psum_t", bufs=1))
         psum_a = ctx.enter_context(tc.psum_pool(name="psum_a", bufs=A_BANKS))
-        psum_b = ctx.enter_context(tc.psum_pool(name="psum_b", bufs=5 - A_BANKS))
+        psum_b = ctx.enter_context(tc.psum_pool(name="psum_b", bufs=6 - A_BANKS))
         psum_v = ctx.enter_context(tc.psum_pool(name="psum_v", bufs=2))
         ctx.enter_context(tc.manual_schedule())
 
@@ -142,7 +141,7 @@ def tile_vae_pb_t_kernel(tc, z, x, Wd1, bd1, Wd2_words, Wd2_scales, bd2, out):
 
         def transpose_z(k, ii):
             if ii == 0:
-                bank = psum_t.tile([P, COLS], BF16, name="zt_ps")
+                bank = psum_b.tile([P, COLS], BF16, name="hb_ps")
                 zt_ps[k] = bank
             nc.tensor.transpose(zt_ps[k][:, ii * P : (ii + 1) * P], z_sb[k][:, ii, :], ident[:])
 
@@ -355,13 +354,16 @@ def tile_vae_pb_t_kernel(tc, z, x, Wd1, bd1, Wd2_words, Wd2_scales, bd2, out):
                     hidden_a(k + 1, q)
             if real(k - 1) and early(k - 1):
                 regroup_early(k - 1)
+            if real(k - 1) and not real(k):
+                quantise(k - 1, GA)
+                quantise(k - 1, GB)
             for q in range(DOTS_A_ROUND if real(k) else DOTS_AT_THE_END):
                 if dotted < TILES and dotted // BLOCK <= ko:
                     dot_with_x(dotted // BLOCK, dotted % BLOCK)
                     dotted += 1
                     if dotted % BLOCK == 0 and dotted // BLOCK - 1 + X_BUFS < BLOCKS:
                         load_x(dotted // BLOCK - 1 + X_BUFS)
-            if real(k - 1):
+            if real(k - 1) and real(k):
                 quantise(k - 1, GA)
                 quantise(k - 1, GB)
             if biased(k) and real(k + 2):

from contextlib import ExitStack

import concourse.mybir as mybir
from concourse.masks import make_identity

F32 = mybir.dt.float32
BF16 = mybir.dt.bfloat16
I32 = mybir.dt.int32
U32 = mybir.dt.uint32
U8 = mybir.dt.uint8
FP8X4 = mybir.dt.float8_e4m3fn_x4
FP4X4 = mybir.dt.float4_e2m1fn_x4
ACT = mybir.ActivationFunctionType
ALU = mybir.AluOpType

P = 128
B, D, L, H = 8192, 512, 128, 1024
PACK = 4
K_PASS = P * PACK
GROUPS = H // K_PASS
TILES = B // P
BLOCK = 4
BLOCKS = TILES // BLOCK
COLS = BLOCK * P
Z_CHUNK = 4
SUPER = 4
LAG_OUT = 2
LAG_EXP = LAG_OUT + SUPER - 1
GA = 0
U_BUFS = 9
A_BANKS = 3
SUPERS = (4, 4, 4, 4)
UNITS_A_ROUND = 4
E_BUFS = 4
EARLY = 5
X_BUFS = 4
DOTS_A_ROUND = 3
DOTS_AT_THE_END = 8
DRAIN = 8
BIASED = 7
GB = 1

FLOPS = 2 * B * L * H + 2 * B * H * D


def tile_vae_pb_t_kernel(tc, z, x, Wd1, bd1, Wd2_words, Wd2_scales, bd2, out):
    nc = tc.nc
    z_rows = z.rearrange("(p i) l -> p i l", i=TILES)
    x_rows = x.rearrange("(p i) j -> p i j", i=TILES)
    out_rows = out.rearrange("(p i) -> p i", i=TILES)

    with ExitStack() as ctx:
        const = ctx.enter_context(tc.tile_pool(name="const", bufs=1))
        work = ctx.enter_context(tc.tile_pool(name="work", bufs=3))
        psum_a = ctx.enter_context(tc.psum_pool(name="psum_a", bufs=A_BANKS))
        psum_b = ctx.enter_context(tc.psum_pool(name="psum_b", bufs=6 - A_BANKS))
        psum_v = ctx.enter_context(tc.psum_pool(name="psum_v", bufs=2))
        ctx.enter_context(tc.manual_schedule())

        w2_scales = const.tile([P, GROUPS, D], U8, align_bytes=64)
        nc.vector.memset(w2_scales[:].bitcast(I32), 0)
        one = const.tile([P, 1], F32)
        nc.vector.memset(one[:], 1.0)
        ident = const.tile([P, P], BF16)
        make_identity(nc, ident[:])

        z_sb = {}
        x_sb = {}

        def load_z(first, blocks):
            z_chunk = const.tile([P, blocks * BLOCK, L], BF16, name="z%d" % first)
            nc.sync.dma_start(out=z_chunk[:], in_=z_rows[:, first * BLOCK : (first + blocks) * BLOCK, :])
            for k in range(first, first + blocks):
                z_sb[k] = z_chunk[:, (k - first) * BLOCK : (k - first + 1) * BLOCK, :]

        def load_x(k):
            x_block = work.tile([P, BLOCK, D], BF16, name="x", bufs=X_BUFS)
            nc.sync.dma_start(out=x_block[:], in_=x_rows[:, k * BLOCK : (k + 1) * BLOCK, :])
            x_sb[k] = x_block

        load_z(0, 1)
        w1_sb = const.tile([P, H], BF16)
        nc.sync.dma_start(out=w1_sb[:], in_=Wd1)
        b1_bf = const.tile([P, GROUPS, PACK], BF16)
        nc.sync.dma_start(out=b1_bf[:], in_=bd1.rearrange("(g p t) -> p g t", g=GROUPS, t=PACK))
        load_z(1, Z_CHUNK - 1)
        b1_line = const.tile([P, K_PASS], BF16)
        nc.sync.dma_start(out=b1_line[0:1, :], in_=bd1[GA * K_PASS : (GA + 1) * K_PASS].rearrange("(o k) -> o k", o=1))
        w2_words = const.tile([P, GROUPS, 2 * D], U8, align_bytes=64)
        for g in range(GROUPS):
            nc.sync.dma_start(out=w2_words[:, g, :].bitcast(I32), in_=Wd2_words[g].bitcast(I32))
        for quad in range(4):
            nc.sync.dma_start(
                out=w2_scales[32 * quad : 32 * quad + 4].bitcast(I32),
                in_=Wd2_scales[:, 4 * quad : 4 * quad + 4, :].bitcast(I32).rearrange("g r n -> r g n"),
            )
        b2_all = const.tile([P, D], BF16)
        nc.sync.dma_start(out=b2_all[:], in_=bd2.partition_broadcast(P))
        for c in range(1, BLOCKS // Z_CHUNK):
            load_x(c - 1)
            load_z(c * Z_CHUNK, Z_CHUNK)
        for k in range(BLOCKS // Z_CHUNK - 1, X_BUFS):
            load_x(k)

        w1_sorted = const.tile([P, GROUPS, PACK, P], BF16)
        for g in range(GROUPS):
            nc.vector.tensor_copy(
                out=w1_sorted[:, g],
                in_=w1_sb[:, g * K_PASS : (g + 1) * K_PASS].rearrange("l (p t) -> l t p", t=PACK),
            )
        b1 = const.tile([P, GROUPS, PACK], F32)
        nc.vector.tensor_copy(out=b1[:], in_=b1_bf[:])

        sum_xu = const.tile([P, TILES], F32)
        sum_softplus = const.tile([P, TILES], F32)

        b1_rows = const.tile([P, P, PACK], F32)
        zeros = const.tile([P, P], F32)
        nc.vector.memset(zeros[:], 0.0)
        for t in range(PACK):
            nc.vector.tensor_scalar_add(out=b1_rows[:, :, t], in0=zeros[:], scalar1=b1[:, GA, t : t + 1])

        bias_w = const.tile([P, PACK, P], BF16)
        nc.vector.memset(bias_w[:], 0.0)
        nc.vector.tensor_copy(out=bias_w[0:1], in_=b1_line[0:1, :].rearrange("o (p t) -> o t p", t=PACK))
        ones_bf = const.tile([P, P], BF16)
        nc.vector.memset(ones_bf[:], 1.0)

        zt_ps = {}
        zT = {}
        ha_ps = {}
        hb_ps = {}
        planes = {}
        planes_a = {}
        grouped = {}
        codes = {}
        scales = {}
        v_ps = {}
        u_sb = {}
        e_sb = {}

        def transpose_z(k, ii):
            if ii == 0:
                bank = psum_b.tile([P, COLS], BF16, name="hb_ps")
                zt_ps[k] = bank
            nc.tensor.transpose(zt_ps[k][:, ii * P : (ii + 1) * P], z_sb[k][:, ii, :], ident[:])

        def copy_zT(k, on_vector):
            zT_block = work.tile([P, COLS], BF16, name="zT")
            if on_vector:
                nc.vector.tensor_copy(out=zT_block[:], in_=zt_ps[k][:])
            else:
                nc.scalar.copy(out=zT_block[:], in_=zt_ps[k][:])
            zT[k] = zT_block

        def hidden_a(k, ii):
            bank = psum_a.tile([P, PACK, P], F32, name="ha_ps")
            for t in range(PACK):
                nc.tensor.matmul(
                    out=bank[:, t, :], lhsT=w1_sorted[:, GA, t, :], rhs=zT[k][:, ii * P : (ii + 1) * P],
                    start=True, stop=not biased(k),
                )
                if biased(k):
                    nc.tensor.matmul(out=bank[:, t, :], lhsT=bias_w[:, t, :], rhs=ones_bf[:], start=False, stop=True)
            ha_ps[(k, ii)] = bank

        def evacuate_a(k, ii):
            if ii == 0:
                words = work.tile([P, COLS, PACK], BF16, name="grouped_a", bufs=3, align_bytes=64)
                grouped[(k, GA)] = words
            if biased(k):
                nc.vector.tensor_scalar_max(
                    out=grouped[(k, GA)][:, ii * P : (ii + 1) * P, :],
                    in0=ha_ps[(k, ii)][:].rearrange("p t c -> p c t"),
                    scalar1=0.0,
                )
            else:
                nc.vector.tensor_tensor(
                    out=grouped[(k, GA)][:, ii * P : (ii + 1) * P, :],
                    in0=ha_ps[(k, ii)][:].rearrange("p t c -> p c t"),
                    in1=b1_rows[:],
                    op=ALU.add,
                )

        def relu_a(k):
            flat = grouped[(k, GA)][:].rearrange("p c t -> p (c t)")
            nc.vector.tensor_scalar_max(out=flat, in0=flat, scalar1=0.0)

        def hidden_b(k, t):
            bank = psum_b.tile([P, COLS], F32, name="hb_ps")
            nc.tensor.matmul(out=bank[:], lhsT=w1_sorted[:, GB, t, :], rhs=zT[k][:], start=True, stop=True)
            hb_ps[(k, t)] = bank

        def evacuate_b(k, t):
            if t == 0:
                four = work.tile([P, PACK, COLS], BF16, name="planes", bufs=2)
                planes[k] = four
            nc.scalar.activation(
                out=planes[k][:, t, :], in_=hb_ps[(k, t)][:], func=ACT.Relu, bias=b1[:, GB, t : t + 1], scale=1.0
            )

        def hidden_early(k, t):
            bank = psum_a.tile([P, COLS], F32, name="ha_ps")
            nc.tensor.matmul(out=bank[:], lhsT=w1_sorted[:, GA, t, :], rhs=zT[k][:], start=True, stop=True)
            ha_ps[(k, t)] = bank

        def evacuate_early(k, t):
            if t == 0:
                four = work.tile([P, PACK, COLS], BF16, name="planes_a", bufs=2)
                planes_a[k] = four
            nc.scalar.activation(
                out=planes_a[k][:, t, :], in_=ha_ps[(k, t)][:], func=ACT.Relu, bias=b1[:, GA, t : t + 1], scale=1.0
            )

        def regroup_early(k):
            words = work.tile([P, COLS, PACK], BF16, name="grouped_a", bufs=3, align_bytes=64)
            grouped[(k, GA)] = words
            nc.vector.tensor_copy(
                out=words[:].rearrange("p (c i) t -> p c t i", i=4),
                in_=planes_a[k][:].rearrange("p t (c i) -> p c t i", i=4),
            )

        def regroup_b(k):
            words = work.tile([P, COLS, PACK], BF16, name="grouped_b", bufs=1, align_bytes=64)
            grouped[(k, GB)] = words
            nc.gpsimd.tensor_scalar(
                out=words[:],
                in0=planes[k][:].rearrange("p t c -> p c t"),
                scalar1=1.0,
                scalar2=0.0,
                op0=ALU.mult,
                op1=ALU.add,
            )

        def quantise(k, g):
            packed = work.tile([P, COLS], U32, name="codes%d" % g, bufs=3, align_bytes=64)
            plane = work.tile([P, COLS], U8, name="scales%d" % g, bufs=3, align_bytes=64)
            nc.vector.quantize_mx(
                out=packed[:].bitcast(FP8X4),
                scales=plane[:],
                in_=grouped[(k, g)][:].rearrange("p c t -> p (c t)"),
            )
            codes[(k, g)] = packed
            scales[(k, g)] = plane

        def output_matmul(k, ii):
            bank = psum_v.tile([P, D], F32, name="v_ps")
            rows = slice(ii * P, (ii + 1) * P)
            for g in range(GROUPS):
                nc.tensor.matmul_mx(
                    out=bank[:],
                    lhsT=codes[(k, g)][:, rows].bitcast(FP8X4),
                    lhsT_scale=scales[(k, g)][:, rows],
                    rhs=w2_words[:, g, :].bitcast(FP4X4),
                    rhs_scale=w2_scales[:, g, :],
                    start=(g == 0),
                    stop=(g == GROUPS - 1),
                )
            v_ps[(k, ii)] = bank

        def add_bias2(k, ii):
            if ii == 0:
                u_block = work.tile([P, BLOCK, D], F32, name="u", bufs=U_BUFS)
                u_sb[k] = u_block
            nc.vector.tensor_tensor(out=u_sb[k][:, ii, :], in0=v_ps[(k, ii)][:], in1=b2_all[:], op=ALU.add)

        def dot_with_x(k, ii):
            product = work.tile([P, D], F32, name="product", bufs=2)
            i = k * BLOCK + ii
            nc.vector.scalar_tensor_tensor(
                out=product[:],
                in0=u_sb[k][:, ii, :],
                scalar=1.0,
                in1=x_sb[k][:, ii, :],
                op0=ALU.mult,
                op1=ALU.mult,
                accum_out=sum_xu[:, i : i + 1],
            )

        def exponential(k, half):
            if half == 0:
                e_block = work.tile([P, BLOCK, D], F32, name="e", bufs=E_BUFS)
                e_sb[k] = e_block
            pair = slice(2 * half, 2 * half + 2)
            nc.scalar.activation(out=e_sb[k][:, pair, :], in_=u_sb[k][:, pair, :], func=ACT.Exp)

        def log1p_sum(k, ii):
            i = k * BLOCK + ii
            nc.scalar.activation(
                out=e_sb[k][:, ii, :],
                in_=e_sb[k][:, ii, :],
                func=ACT.Ln,
                bias=one[:, 0:1],
                scale=1.0,
                accum_out=sum_softplus[:, i : i + 1],
            )

        def real(k):
            return 0 <= k < BLOCKS

        def early(k):
            return k < EARLY

        def biased(k):
            return k >= BLOCKS - BIASED

        units = []
        first = 0
        for size in SUPERS:
            for b in range(first, first + size):
                units.extend([("exp", b, 0), ("exp", b, 1)])
            for b in range(first, first + size):
                units.extend([("ln", b, 0), ("ln", b, 1)])
            first += size

        taken = 0
        dotted = 0
        for k in range(-2, BLOCKS + DRAIN):
            ko = k - LAG_OUT
            late = real(k) and not early(k)
            if real(k - 1):
                regroup_b(k - 1)
            for q in range(UNITS_A_ROUND):
                if taken < len(units) and units[taken][1] < ko:
                    kind, b, half = units[taken]
                    taken += 1
                    if kind == "exp":
                        exponential(b, half)
                    else:
                        log1p_sum(b, 2 * half)
                        log1p_sum(b, 2 * half + 1)
            if real(ko):
                output_matmul(ko, 0)
                output_matmul(ko, 1)
            if late:
                evacuate_a(k, 0)
                hidden_a(k, 3)
                evacuate_a(k, 1)
                evacuate_a(k, 2)
            if real(ko):
                add_bias2(ko, 0)
                output_matmul(ko, 2)
                add_bias2(ko, 1)
                output_matmul(ko, 3)
            if late:
                evacuate_a(k, 3)
            if real(ko):
                add_bias2(ko, 2)
                add_bias2(ko, 3)
            if late and not biased(k):
                relu_a(k)
            if real(k + 1) and not early(k):
                for q in range(A_BANKS - 1):
                    hidden_a(k + 1, q)
            if real(k - 1) and early(k - 1):
                regroup_early(k - 1)
            if real(k - 1) and not real(k):
                quantise(k - 1, GA)
                quantise(k - 1, GB)
            for q in range(DOTS_A_ROUND if real(k) else DOTS_AT_THE_END):
                if dotted < TILES and dotted // BLOCK <= ko:
                    dot_with_x(dotted // BLOCK, dotted % BLOCK)
                    dotted += 1
                    if dotted % BLOCK == 0 and dotted // BLOCK - 1 + X_BUFS < BLOCKS:
                        load_x(dotted // BLOCK - 1 + X_BUFS)
            if real(k - 1) and real(k):
                quantise(k - 1, GA)
                quantise(k - 1, GB)
            if biased(k) and real(k + 2):
                for q in range(4):
                    transpose_z(k + 2, q)
                copy_zT(k + 2, True)
            for t in range(PACK):
                if real(k):
                    if early(k):
                        hidden_early(k, t)
                        evacuate_early(k, t)
                    hidden_b(k, t)
                    evacuate_b(k, t)
            for kz in (k + 2,) if k != -1 and k != 0 else (1, 2) if k == 0 else ():
                if real(kz) and not biased(k):
                    for q in range(4):
                        transpose_z(kz, q)
                    copy_zT(kz, False)
            if real(k + 1) and not early(k + 1):
                for q in range(A_BANKS - 1 if not early(k) else 0, A_BANKS):
                    hidden_a(k + 1, q)
        assert taken == len(units) and dotted == TILES

        result = const.tile([P, TILES], F32)
        nc.vector.tensor_sub(out=result[:], in0=sum_xu[:], in1=sum_softplus[:])
        nc.sync.dma_start(out=out_rows, in_=result[:])
